import numpy as np
import ml_dtypes


def mxq(x, axis, fmt="e4m3"):
    dtype, down = {"e4m3": (ml_dtypes.float8_e4m3fn, 7), "e5m2": (ml_dtypes.float8_e5m2, 14)}[fmt]
    v = np.moveaxis(np.asarray(x, np.float32).astype(ml_dtypes.bfloat16).astype(np.float64), axis, -1)
    blocks = v.reshape(v.shape[:-1] + (-1, 32))
    amax = np.abs(blocks).max(-1, keepdims=True)
    byte = np.maximum(np.where(amax > 0, np.frexp(amax)[1] - 1 + 127, 0) - down, 1)
    scale = np.exp2(byte - 127.0)
    codes = (blocks / scale).astype(np.float32).astype(dtype).astype(np.float64)
    return np.moveaxis((codes * scale).reshape(v.shape), -1, axis)


WIDE = False


def mx_kscale(k):
    if not WIDE:
        return np.ones(k)
    levels = np.array([10, -10, 5, -5, 0])
    a = np.random.permutation(np.resize(levels, k // 512 * 4)).reshape(k // 512, 4)
    idx = np.arange(k)
    return np.exp2(a[idx // 512, idx % 128 // 32])


BF16 = ml_dtypes.bfloat16


def bf(x):
    return np.asarray(x, np.float32).astype(BF16)


def f64(x):
    return np.asarray(x).astype(np.float64)


E2M1 = np.array([0.0, 0.5, 1.0, 1.5, 2.0, 3.0, 4.0, 6.0, -0.0, -0.5, -1.0, -1.5, -2.0, -3.0, -4.0, -6.0])


def pack_weight(w, fmt):
    k, n = w.shape
    w = f64(bf(w)).reshape(k // 32, 32, n)
    amax = np.abs(w).max(1)
    if fmt == "e4m3":
        byte = np.frexp(amax)[1] - 1 + 127 - 7
    else:
        mant, ex = np.frexp(amax / 6.0)
        byte = np.where(mant > 0.5, ex, ex - 1) + 127
    byte = np.clip(np.where(amax > 0, byte, 1), 1, 254)
    scaled = (w * np.exp2(127.0 - byte)[:, None, :]).reshape(k, n).astype(np.float32)
    by_word = np.ascontiguousarray(scaled.reshape(k // 512, 128, 4, n).transpose(0, 1, 3, 2))
    if fmt == "e4m3":
        words = by_word.astype(ml_dtypes.float8_e4m3fn).view(np.uint8)
    else:
        c = by_word.astype(ml_dtypes.float4_e2m1fn).view(np.uint8) & 0xF
        words = c[..., 0::2] | (c[..., 1::2] << 4)
    return np.ascontiguousarray(words), np.ascontiguousarray(byte.astype(np.uint8).reshape(k // 512, 16, n))


def unpack_weight(words, scales, fmt):
    g, p, n, _ = words.shape
    if fmt == "e4m3":
        vals = np.ascontiguousarray(words).view(ml_dtypes.float8_e4m3fn).astype(np.float64)
    else:
        nib = np.empty((g, p, n, 4), np.uint8)
        nib[..., 0::2] = words & 0xF
        nib[..., 1::2] = words >> 4
        vals = E2M1[nib]
    vals = vals * np.repeat(np.exp2(scales.astype(np.float64) - 127.0), 8, axis=1)[..., None]
    return vals.transpose(0, 1, 3, 2).reshape(g * 512, n)


B, H, E, V = 128, 512, 16384, 4096
FMT = "e4m3"


def sigmoid(v):
    return 1.0 / (1.0 + np.exp(-v))


def draw_w(k, n, div):
    return pack_weight(np.random.standard_normal((k, n)) / np.sqrt(k) / div[:, None], FMT)


def setup_inputs():
    s, t = mx_kscale(E), mx_kscale(H)
    one = np.ones(H)
    inputs = {
        "input_data": bf(np.random.standard_normal((B, E)) * s),
        "previous_hidden_state": bf(np.random.standard_normal((B, H)) * t),
        "previous_c_state": bf(np.random.standard_normal((B, H))),
    }
    for name, k, div in (
        ("w_forget", H, t),
        ("w_input", H, t),
        ("w_c_dash", H, t),
        ("w_forget_c", H, one),
        ("w_input_c", H, one),
        ("w_ip_f", E, s),
        ("w_ip_i", E, s),
        ("w_ip_c_dash", E, s),
    ):
        words, scales = draw_w(k, H, div)
        inputs[name + "_words"] = words
        inputs[name + "_scales"] = scales
    return inputs


def reference(input_data, previous_hidden_state, previous_c_state,
              w_forget_words, w_forget_scales, w_input_words, w_input_scales,
              w_c_dash_words, w_c_dash_scales, w_forget_c_words, w_forget_c_scales,
              w_input_c_words, w_input_c_scales, w_ip_f_words, w_ip_f_scales,
              w_ip_i_words, w_ip_i_scales, w_ip_c_dash_words, w_ip_c_dash_scales):
    c = f64(previous_c_state)
    xq = mxq(f64(input_data), 1, "e4m3")
    hq = mxq(f64(previous_hidden_state), 1, "e4m3")
    cq = mxq(c, 1, "e4m3")
    zf = (xq @ unpack_weight(w_ip_f_words, w_ip_f_scales, FMT)) + (hq @ unpack_weight(w_forget_words, w_forget_scales, FMT))
    zi = (xq @ unpack_weight(w_ip_i_words, w_ip_i_scales, FMT)) + (hq @ unpack_weight(w_input_words, w_input_scales, FMT))
    zc = (xq @ unpack_weight(w_ip_c_dash_words, w_ip_c_dash_scales, FMT)) + (hq @ unpack_weight(w_c_dash_words, w_c_dash_scales, FMT))
    ft = sigmoid(zf + (cq @ unpack_weight(w_forget_c_words, w_forget_c_scales, FMT)))
    it = sigmoid(zi + (cq @ unpack_weight(w_input_c_words, w_input_c_scales, FMT)))
    ct_dash = np.tanh(zc)
    return ft * c + it * ct_dash

@@ -1,0 +1,178 @@
+import concourse.mybir as mybir
+from concourse.masks import make_identity
+
+BF16 = mybir.dt.bfloat16
+F32 = mybir.dt.float32
+I32 = mybir.dt.int32
+U32 = mybir.dt.uint32
+U8 = mybir.dt.uint8
+FP8X4 = mybir.dt.float8_e4m3fn_x4
+ACT = mybir.ActivationFunctionType
+
+P = 128
+K_PASS = 512
+B = 128
+H = 512
+E = 16384
+
+X_GROUPS = E // K_PASS
+H_GROUP = X_GROUPS
+C_GROUP = X_GROUPS + 1
+ACT_GROUPS = X_GROUPS + 2
+X_LOADS = 4
+
+WORDS_PER_GROUP = K_PASS // 2
+CHUNK = 4
+STREAM_BUFS = 12
+
+F_OFFSET, I_OFFSET, C_OFFSET, SMALL_OFFSET = 0, 4, 8, 12
+
+FLOPS = 2 * B * H * (3 * E + 5 * H)
+
+
+def load_scale_rows(nc, planes, offset, scales):
+    groups = scales.shape[0]
+    rows = scales.bitcast(F32).rearrange("g (q r) n -> r q g n", r=4)
+    for r in range(4):
+        nc.gpsimd.dma_start(
+            out=planes[offset + r : P : 32, 0:groups, :].bitcast(F32),
+            in_=rows[r],
+        )
+
+
+def mx_pass(nc, z, act_codes, act_scales, group, words, plane, start, stop):
+    batch_cols = slice(group * B, (group + 1) * B)
+    nc.tensor.matmul_mx(
+        out=z[:],
+        lhsT=act_codes[:, batch_cols].bitcast(FP8X4),
+        lhsT_scale=act_scales[:, batch_cols],
+        rhs=words.bitcast(FP8X4),
+        rhs_scale=plane,
+        start=start,
+        stop=stop,
+    )
+
+
+def stream_x_product(nc, stream, z, words, planes, offset, act_codes, act_scales, start, stop):
+    by_partition = words.rearrange("g p n t -> p g (n t)").bitcast(I32)
+    for first in range(0, X_GROUPS, CHUNK):
+        w_sb = stream.tile([P, CHUNK, H], U32, align_bytes=64)
+        nc.sync.dma_start(out=w_sb[:].bitcast(I32), in_=by_partition[:, first : first + CHUNK, :])
+        for j in range(CHUNK):
+            group = first + j
+            mx_pass(
+                nc, z, act_codes, act_scales, group, w_sb[:, j, :], planes[offset:P, group, :],
+                start=start and group == 0,
+                stop=stop and group == X_GROUPS - 1,
+            )
+
+
+def tile_lstm_peephole_build_pa_k_kernel(
+    tc,
+    input_data, previous_hidden_state, previous_c_state,
+    w_forget_words, w_forget_scales, w_input_words, w_input_scales,
+    w_c_dash_words, w_c_dash_scales, w_forget_c_words, w_forget_c_scales,
+    w_input_c_words, w_input_c_scales, w_ip_f_words, w_ip_f_scales,
+    w_ip_i_words, w_ip_i_scales, w_ip_c_dash_words, w_ip_c_dash_scales,
+    out,
+):
+    nc = tc.nc
+    FORGET_H, FORGET_C, INPUT_H, INPUT_C, DASH_H = range(5)
+    small_words_in = (w_forget_words, w_forget_c_words, w_input_words, w_input_c_words, w_c_dash_words)
+    small_scales_in = (w_forget_scales, w_forget_c_scales, w_input_scales, w_input_c_scales, w_c_dash_scales)
+
+    with tc.tile_pool(name="keep", bufs=1) as keep, \
+            tc.tile_pool(name="stage", bufs=4) as stage, \
+            tc.tile_pool(name="stream", bufs=STREAM_BUFS) as stream, \
+            tc.psum_pool(name="sums", bufs=1) as sums, \
+            tc.psum_pool(name="turn", bufs=4) as turn:
+
+        acts = keep.tile([P, ACT_GROUPS * K_PASS], BF16, align_bytes=64)
+        x_cols = E // X_LOADS
+        for i in range(X_LOADS):
+            cols = slice(i * x_cols, (i + 1) * x_cols)
+            nc.sync.dma_start(out=acts[:, cols], in_=input_data[:, cols])
+        h_cols = slice(H_GROUP * K_PASS, (H_GROUP + 1) * K_PASS)
+        c_cols = slice(C_GROUP * K_PASS, (C_GROUP + 1) * K_PASS)
+        nc.sync.dma_start(out=acts[:, h_cols], in_=previous_hidden_state)
+        nc.sync.dma_start(out=acts[:, c_cols], in_=previous_c_state)
+
+        planes = keep.tile([P, X_GROUPS, H], U8, align_bytes=64)
+        nc.vector.memset(planes[:].bitcast(I32), 0)
+        ident = keep.tile([P, P], F32)
+        make_identity(nc, ident[:])
+        load_scale_rows(nc, planes, F_OFFSET, w_ip_f_scales)
+        load_scale_rows(nc, planes, I_OFFSET, w_ip_i_scales)
+        load_scale_rows(nc, planes, C_OFFSET, w_ip_c_dash_scales)
+        for slot, scales in enumerate(small_scales_in):
+            load_scale_rows(nc, planes[:, slot : slot + 1, :], SMALL_OFFSET, scales)
+
+        act_words = acts[:].bitcast(F32)
+        act_codes = keep.tile([P, ACT_GROUPS * B], U32, align_bytes=64)
+        act_scales = keep.tile([P, ACT_GROUPS * B], U8, align_bytes=64)
+        for pair in range(ACT_GROUPS // 2):
+            turned = turn.tile([P, 2, 2, B], F32)
+            for gg in range(2):
+                first_word = (2 * pair + gg) * WORDS_PER_GROUP
+                for u in range(2):
+                    nc.tensor.transpose(
+                        turned[:, gg, u, :],
+                        act_words[:, first_word + u : first_word + WORDS_PER_GROUP : 2],
+                        ident[:],
+                    )
+            grouped = stage.tile([P, 2 * K_PASS], BF16, align_bytes=64)
+            copy_out = nc.vector.tensor_copy if pair % 2 == 0 else nc.scalar.copy
+            copy_out(
+                out=grouped[:].bitcast(F32).rearrange("p (gg b u) -> p gg b u", gg=2, u=2),
+                in_=turned[:].rearrange("p gg u b -> p gg b u"),
+            )
+            pair_cols = slice(2 * pair * B, (2 * pair + 2) * B)
+            nc.vector.quantize_mx(
+                out=act_codes[:, pair_cols].bitcast(FP8X4),
+                scales=act_scales[:, pair_cols],
+                in_=grouped[:],
+            )
+
+        z_f = sums.tile([B, H], F32)
+        z_i = sums.tile([B, H], F32)
+        z_c = sums.tile([B, H], F32)
+        stream_x_product(nc, stream, z_f, w_ip_f_words, planes, F_OFFSET, act_codes, act_scales,
+                         start=True, stop=False)
+        stream_x_product(nc, stream, z_i, w_ip_i_words, planes, I_OFFSET, act_codes, act_scales,
+                         start=True, stop=False)
+
+        small_words = keep.tile([P, len(small_words_in), H], U32, align_bytes=64)
+        for slot, words in enumerate(small_words_in):
+            nc.sync.dma_start(
+                out=small_words[:, slot, :].bitcast(I32),
+                in_=words.rearrange("g p n t -> p (g n t)").bitcast(I32),
+            )
+
+        def small_pass(z, group, slot, start, stop):
+            mx_pass(
+                nc, z, act_codes, act_scales, group, small_words[:, slot, :],
+                planes[SMALL_OFFSET:P, slot, :], start=start, stop=stop,
+            )
+
+        small_pass(z_f, H_GROUP, FORGET_H, start=False, stop=False)
+        small_pass(z_f, C_GROUP, FORGET_C, start=False, stop=True)
+        small_pass(z_i, H_GROUP, INPUT_H, start=False, stop=False)
+        small_pass(z_i, C_GROUP, INPUT_C, start=False, stop=True)
+
+        forget = keep.tile([B, H], F32)
+        nc.scalar.activation(out=forget[:], in_=z_f[:], func=ACT.Sigmoid)
+        kept = keep.tile([B, H], F32)
+        nc.vector.tensor_mul(out=kept[:], in0=forget[:], in1=acts[:, c_cols])
+        admit = keep.tile([B, H], F32)
+        nc.scalar.activation(out=admit[:], in_=z_i[:], func=ACT.Sigmoid)
+
+        small_pass(z_c, H_GROUP, DASH_H, start=True, stop=False)
+        stream_x_product(nc, stream, z_c, w_ip_c_dash_words, planes, C_OFFSET, act_codes, act_scales,
+                         start=False, stop=True)
+
+        fresh = keep.tile([B, H], F32)
+        nc.scalar.activation(out=fresh[:], in_=z_c[:], func=ACT.Tanh)
+        result = keep.tile([B, H], F32)
+        nc.vector.tensor_mul(out=result[:], in0=admit[:], in1=fresh[:])
+        nc.vector.tensor_add(out=result[:], in0=result[:], in1=kept[:])
+        nc.sync.dma_start(out=out, in_=result[:])

@@ -23,21 +23,16 @@ X_LOADS = 4
 
 WORDS_PER_GROUP = K_PASS // 2
 CHUNK = 4
-STREAM_BUFS = 12
-
-F_OFFSET, I_OFFSET, C_OFFSET, SMALL_OFFSET = 0, 4, 8, 12
+STREAM_BUFS = 10
 
 FLOPS = 2 * B * H * (3 * E + 5 * H)
 
 
-def load_scale_rows(nc, planes, offset, scales):
-    groups = scales.shape[0]
+def load_scale_planes(nc, planes, scales):
+    nc.vector.memset(planes[:].bitcast(I32), 0)
     rows = scales.bitcast(F32).rearrange("g (q r) n -> r q g n", r=4)
     for r in range(4):
-        nc.gpsimd.dma_start(
-            out=planes[offset + r : P : 32, 0:groups, :].bitcast(F32),
-            in_=rows[r],
-        )
+        nc.gpsimd.dma_start(out=planes[r : P : 32, :, :].bitcast(F32), in_=rows[r])
 
 
 def mx_pass(nc, z, act_codes, act_scales, group, words, plane, start, stop):
@@ -53,15 +48,16 @@ def mx_pass(nc, z, act_codes, act_scales, group, words, plane, start, stop):
     )
 
 
-def stream_x_product(nc, stream, z, words, planes, offset, act_codes, act_scales, start, stop):
+def stream_x_product(nc, stream, z, words, planes, act_codes, act_scales, chunks, start, stop):
     by_partition = words.rearrange("g p n t -> p g (n t)").bitcast(I32)
-    for first in range(0, X_GROUPS, CHUNK):
+    for chunk in chunks:
+        first = chunk * CHUNK
         w_sb = stream.tile([P, CHUNK, H], U32, align_bytes=64)
         nc.sync.dma_start(out=w_sb[:].bitcast(I32), in_=by_partition[:, first : first + CHUNK, :])
         for j in range(CHUNK):
             group = first + j
             mx_pass(
-                nc, z, act_codes, act_scales, group, w_sb[:, j, :], planes[offset:P, group, :],
+                nc, z, act_codes, act_scales, group, w_sb[:, j, :], planes[:, group, :],
                 start=start and group == 0,
                 stop=stop and group == X_GROUPS - 1,
             )
@@ -97,15 +93,18 @@ def tile_lstm_peephole_build_pa_k_kernel(
         nc.sync.dma_start(out=acts[:, h_cols], in_=previous_hidden_state)
         nc.sync.dma_start(out=acts[:, c_cols], in_=previous_c_state)
 
-        planes = keep.tile([P, X_GROUPS, H], U8, align_bytes=64)
-        nc.vector.memset(planes[:].bitcast(I32), 0)
         ident = keep.tile([P, P], F32)
         make_identity(nc, ident[:])
-        load_scale_rows(nc, planes, F_OFFSET, w_ip_f_scales)
-        load_scale_rows(nc, planes, I_OFFSET, w_ip_i_scales)
-        load_scale_rows(nc, planes, C_OFFSET, w_ip_c_dash_scales)
+        f_planes = keep.tile([P, X_GROUPS, H], U8, align_bytes=64)
+        i_planes = keep.tile([P, X_GROUPS, H], U8, align_bytes=64)
+        c_planes = keep.tile([P, X_GROUPS, H], U8, align_bytes=64)
+        load_scale_planes(nc, f_planes, w_ip_f_scales)
+        load_scale_planes(nc, i_planes, w_ip_i_scales)
+        load_scale_planes(nc, c_planes, w_ip_c_dash_scales)
+        small_planes = []
         for slot, scales in enumerate(small_scales_in):
-            load_scale_rows(nc, planes[:, slot : slot + 1, :], SMALL_OFFSET, scales)
+            small_planes.append(keep.tile([P, 1, H], U8, name="small_plane%d" % slot, align_bytes=64))
+            load_scale_planes(nc, small_planes[slot], scales)
 
         act_words = acts[:].bitcast(F32)
         act_codes = keep.tile([P, ACT_GROUPS * B], U32, align_bytes=64)
@@ -133,13 +132,14 @@ def tile_lstm_peephole_build_pa_k_kernel(
                 in_=grouped[:],
             )
 
+        all_chunks = range(X_GROUPS // CHUNK)
         z_f = sums.tile([B, H], F32)
         z_i = sums.tile([B, H], F32)
         z_c = sums.tile([B, H], F32)
-        stream_x_product(nc, stream, z_f, w_ip_f_words, planes, F_OFFSET, act_codes, act_scales,
-                         start=True, stop=False)
-        stream_x_product(nc, stream, z_i, w_ip_i_words, planes, I_OFFSET, act_codes, act_scales,
-                         start=True, stop=False)
+        stream_x_product(nc, stream, z_f, w_ip_f_words, f_planes, act_codes, act_scales,
+                         all_chunks, start=True, stop=False)
+        stream_x_product(nc, stream, z_i, w_ip_i_words, i_planes, act_codes, act_scales,
+                         all_chunks, start=True, stop=False)
 
         small_words = keep.tile([P, len(small_words_in), H], U32, align_bytes=64)
         for slot, words in enumerate(small_words_in):
@@ -151,8 +151,11 @@ def tile_lstm_peephole_build_pa_k_kernel(
         def small_pass(z, group, slot, start, stop):
             mx_pass(
                 nc, z, act_codes, act_scales, group, small_words[:, slot, :],
-                planes[SMALL_OFFSET:P, slot, :], start=start, stop=stop,
+                small_planes[slot][:, 0, :], start=start, stop=stop,
             )
+
+        stream_x_product(nc, stream, z_c, w_ip_c_dash_words, c_planes, act_codes, act_scales,
+                         all_chunks[:-1], start=True, stop=False)
 
         small_pass(z_f, H_GROUP, FORGET_H, start=False, stop=False)
         small_pass(z_f, C_GROUP, FORGET_C, start=False, stop=True)
@@ -166,9 +169,9 @@ def tile_lstm_peephole_build_pa_k_kernel(
         admit = keep.tile([B, H], F32)
         nc.scalar.activation(out=admit[:], in_=z_i[:], func=ACT.Sigmoid)
 
-        small_pass(z_c, H_GROUP, DASH_H, start=True, stop=False)
-        stream_x_product(nc, stream, z_c, w_ip_c_dash_words, planes, C_OFFSET, act_codes, act_scales,
-                         start=False, stop=True)
+        small_pass(z_c, H_GROUP, DASH_H, start=False, stop=False)
+        stream_x_product(nc, stream, z_c, w_ip_c_dash_words, c_planes, act_codes, act_scales,
+                         all_chunks[-1:], start=False, stop=True)
 
         fresh = keep.tile([B, H], F32)
         nc.scalar.activation(out=fresh[:], in_=z_c[:], func=ACT.Tanh)

@@ -23,16 +23,17 @@ X_LOADS = 4
 
 WORDS_PER_GROUP = K_PASS // 2
 CHUNK = 4
-STREAM_BUFS = 10
+STREAM_BUFS = 12
+
+F_OFFSET, I_OFFSET, C_OFFSET, SMALL_OFFSET = 0, 4, 8, 12
 
 FLOPS = 2 * B * H * (3 * E + 5 * H)
 
 
-def load_scale_planes(nc, planes, scales):
-    nc.vector.memset(planes[:].bitcast(I32), 0)
+def load_scale_planes(nc, planes, offset, scales):
     rows = scales.bitcast(F32).rearrange("g (q r) n -> r q g n", r=4)
     for r in range(4):
-        nc.gpsimd.dma_start(out=planes[r : P : 32, :, :].bitcast(F32), in_=rows[r])
+        nc.gpsimd.dma_start(out=planes[offset + r : P : 32, :, :].bitcast(F32), in_=rows[r])
 
 
 def mx_pass(nc, z, act_codes, act_scales, group, words, plane, start, stop):
@@ -48,7 +49,7 @@ def mx_pass(nc, z, act_codes, act_scales, group, words, plane, start, stop):
     )
 
 
-def stream_x_product(nc, stream, z, words, planes, act_codes, act_scales, chunks, start, stop):
+def stream_x_product(nc, stream, z, words, planes, offset, act_codes, act_scales, chunks, start, stop):
     by_partition = words.rearrange("g p n t -> p g (n t)").bitcast(I32)
     for chunk in chunks:
         first = chunk * CHUNK
@@ -57,7 +58,7 @@ def stream_x_product(nc, stream, z, words, planes, act_codes, act_scales, chunks
         for j in range(CHUNK):
             group = first + j
             mx_pass(
-                nc, z, act_codes, act_scales, group, w_sb[:, j, :], planes[:, group, :],
+                nc, z, act_codes, act_scales, group, w_sb[:, j, :], planes[offset:P, group, :],
                 start=start and group == 0,
                 stop=stop and group == X_GROUPS - 1,
             )
@@ -95,16 +96,15 @@ def tile_lstm_peephole_build_pa_k_kernel(
 
         ident = keep.tile([P, P], F32)
         make_identity(nc, ident[:])
-        f_planes = keep.tile([P, X_GROUPS, H], U8, align_bytes=64)
-        i_planes = keep.tile([P, X_GROUPS, H], U8, align_bytes=64)
-        c_planes = keep.tile([P, X_GROUPS, H], U8, align_bytes=64)
-        load_scale_planes(nc, f_planes, w_ip_f_scales)
-        load_scale_planes(nc, i_planes, w_ip_i_scales)
-        load_scale_planes(nc, c_planes, w_ip_c_dash_scales)
-        small_planes = []
+        big_planes = keep.tile([P, X_GROUPS, H], U8, align_bytes=64)
+        small_planes = keep.tile([P, len(small_scales_in), H], U8, align_bytes=64)
+        nc.vector.memset(big_planes[:].bitcast(I32), 0)
+        nc.vector.memset(small_planes[:].bitcast(I32), 0)
+        load_scale_planes(nc, big_planes, F_OFFSET, w_ip_f_scales)
+        load_scale_planes(nc, big_planes, I_OFFSET, w_ip_i_scales)
+        load_scale_planes(nc, big_planes, C_OFFSET, w_ip_c_dash_scales)
         for slot, scales in enumerate(small_scales_in):
-            small_planes.append(keep.tile([P, 1, H], U8, name="small_plane%d" % slot, align_bytes=64))
-            load_scale_planes(nc, small_planes[slot], scales)
+            load_scale_planes(nc, small_planes[:, slot : slot + 1, :], SMALL_OFFSET, scales)
 
         act_words = acts[:].bitcast(F32)
         act_codes = keep.tile([P, ACT_GROUPS * B], U32, align_bytes=64)
@@ -136,9 +136,9 @@ def tile_lstm_peephole_build_pa_k_kernel(
         z_f = sums.tile([B, H], F32)
         z_i = sums.tile([B, H], F32)
         z_c = sums.tile([B, H], F32)
-        stream_x_product(nc, stream, z_f, w_ip_f_words, f_planes, act_codes, act_scales,
+        stream_x_product(nc, stream, z_f, w_ip_f_words, big_planes, F_OFFSET, act_codes, act_scales,
                          all_chunks, start=True, stop=False)
-        stream_x_product(nc, stream, z_i, w_ip_i_words, i_planes, act_codes, act_scales,
+        stream_x_product(nc, stream, z_i, w_ip_i_words, big_planes, I_OFFSET, act_codes, act_scales,
                          all_chunks, start=True, stop=False)
 
         small_words = keep.tile([P, len(small_words_in), H], U32, align_bytes=64)
@@ -151,10 +151,10 @@ def tile_lstm_peephole_build_pa_k_kernel(
         def small_pass(z, group, slot, start, stop):
             mx_pass(
                 nc, z, act_codes, act_scales, group, small_words[:, slot, :],
-                small_planes[slot][:, 0, :], start=start, stop=stop,
+                small_planes[SMALL_OFFSET:P, slot, :], start=start, stop=stop,
             )
 
-        stream_x_product(nc, stream, z_c, w_ip_c_dash_words, c_planes, act_codes, act_scales,
+        stream_x_product(nc, stream, z_c, w_ip_c_dash_words, big_planes, C_OFFSET, act_codes, act_scales,
                          all_chunks[:-1], start=True, stop=False)
 
         small_pass(z_f, H_GROUP, FORGET_H, start=False, stop=False)
@@ -170,7 +170,7 @@ def tile_lstm_peephole_build_pa_k_kernel(
         nc.scalar.activation(out=admit[:], in_=z_i[:], func=ACT.Sigmoid)
 
         small_pass(z_c, H_GROUP, DASH_H, start=False, stop=False)
-        stream_x_product(nc, stream, z_c, w_ip_c_dash_words, c_planes, act_codes, act_scales,
+        stream_x_product(nc, stream, z_c, w_ip_c_dash_words, big_planes, C_OFFSET, act_codes, act_scales,
                          all_chunks[-1:], start=False, stop=True)
 
         fresh = keep.tile([B, H], F32)

@@ -23,17 +23,17 @@ X_LOADS = 4
 
 WORDS_PER_GROUP = K_PASS // 2
 CHUNK = 4
-STREAM_BUFS = 12
+STREAM_BUFS = 10
 
 F_OFFSET, I_OFFSET, C_OFFSET, SMALL_OFFSET = 0, 4, 8, 12
 
 FLOPS = 2 * B * H * (3 * E + 5 * H)
 
 
-def load_scale_planes(nc, planes, offset, scales):
-    rows = scales.bitcast(F32).rearrange("g (q r) n -> r q g n", r=4)
+def load_scale_planes(queue, word, planes, offset, scales):
+    rows = scales.bitcast(word).rearrange("g (q r) n -> r q g n", r=4)
     for r in range(4):
-        nc.gpsimd.dma_start(out=planes[offset + r : P : 32, :, :].bitcast(F32), in_=rows[r])
+        queue.dma_start(out=planes[offset + r : P : 32, :, :].bitcast(word), in_=rows[r])
 
 
 def mx_pass(nc, z, act_codes, act_scales, group, words, plane, start, stop):
@@ -94,17 +94,19 @@ def tile_lstm_peephole_build_pa_k_kernel(
         nc.sync.dma_start(out=acts[:, h_cols], in_=previous_hidden_state)
         nc.sync.dma_start(out=acts[:, c_cols], in_=previous_c_state)
 
+        small_planes = keep.tile([P, len(small_scales_in), H], U8, align_bytes=64)
+        f_planes = keep.tile([P, X_GROUPS, H], U8, align_bytes=64)
+        i_planes = keep.tile([P, X_GROUPS, H], U8, align_bytes=64)
+        c_planes = keep.tile([P, X_GROUPS, H], U8, align_bytes=64)
+        for planes in (small_planes, f_planes, i_planes, c_planes):
+            nc.vector.memset(planes[:].bitcast(I32), 0)
+        for slot, scales in enumerate(small_scales_in):
+            load_scale_planes(nc.sync, I32, small_planes[:, slot : slot + 1, :], SMALL_OFFSET, scales)
         ident = keep.tile([P, P], F32)
         make_identity(nc, ident[:])
-        big_planes = keep.tile([P, X_GROUPS, H], U8, align_bytes=64)
-        small_planes = keep.tile([P, len(small_scales_in), H], U8, align_bytes=64)
-        nc.vector.memset(big_planes[:].bitcast(I32), 0)
-        nc.vector.memset(small_planes[:].bitcast(I32), 0)
-        load_scale_planes(nc, big_planes, F_OFFSET, w_ip_f_scales)
-        load_scale_planes(nc, big_planes, I_OFFSET, w_ip_i_scales)
-        load_scale_planes(nc, big_planes, C_OFFSET, w_ip_c_dash_scales)
-        for slot, scales in enumerate(small_scales_in):
-            load_scale_planes(nc, small_planes[:, slot : slot + 1, :], SMALL_OFFSET, scales)
+        load_scale_planes(nc.gpsimd, F32, f_planes, F_OFFSET, w_ip_f_scales)
+        load_scale_planes(nc.gpsimd, F32, i_planes, I_OFFSET, w_ip_i_scales)
+        load_scale_planes(nc.gpsimd, F32, c_planes, C_OFFSET, w_ip_c_dash_scales)
 
         act_words = acts[:].bitcast(F32)
         act_codes = keep.tile([P, ACT_GROUPS * B], U32, align_bytes=64)
@@ -136,9 +138,9 @@ def tile_lstm_peephole_build_pa_k_kernel(
         z_f = sums.tile([B, H], F32)
         z_i = sums.tile([B, H], F32)
         z_c = sums.tile([B, H], F32)
-        stream_x_product(nc, stream, z_f, w_ip_f_words, big_planes, F_OFFSET, act_codes, act_scales,
+        stream_x_product(nc, stream, z_f, w_ip_f_words, f_planes, F_OFFSET, act_codes, act_scales,
                          all_chunks, start=True, stop=False)
-        stream_x_product(nc, stream, z_i, w_ip_i_words, big_planes, I_OFFSET, act_codes, act_scales,
+        stream_x_product(nc, stream, z_i, w_ip_i_words, i_planes, I_OFFSET, act_codes, act_scales,
                          all_chunks, start=True, stop=False)
 
         small_words = keep.tile([P, len(small_words_in), H], U32, align_bytes=64)
@@ -154,7 +156,7 @@ def tile_lstm_peephole_build_pa_k_kernel(
                 small_planes[SMALL_OFFSET:P, slot, :], start=start, stop=stop,
             )
 
-        stream_x_product(nc, stream, z_c, w_ip_c_dash_words, big_planes, C_OFFSET, act_codes, act_scales,
+        stream_x_product(nc, stream, z_c, w_ip_c_dash_words, c_planes, C_OFFSET, act_codes, act_scales,
                          all_chunks[:-1], start=True, stop=False)
 
         small_pass(z_f, H_GROUP, FORGET_H, start=False, stop=False)
@@ -170,7 +172,7 @@ def tile_lstm_peephole_build_pa_k_kernel(
         nc.scalar.activation(out=admit[:], in_=z_i[:], func=ACT.Sigmoid)
 
         small_pass(z_c, H_GROUP, DASH_H, start=False, stop=False)
-        stream_x_product(nc, stream, z_c, w_ip_c_dash_words, big_planes, C_OFFSET, act_codes, act_scales,
+        stream_x_product(nc, stream, z_c, w_ip_c_dash_words, c_planes, C_OFFSET, act_codes, act_scales,
                          all_chunks[-1:], start=False, stop=True)
 
         fresh = keep.tile([B, H], F32)

@@ -23,45 +23,19 @@ X_LOADS = 4
 
 WORDS_PER_GROUP = K_PASS // 2
 CHUNK = 4
+LOADS_PER_WEIGHT = X_GROUPS // CHUNK
 STREAM_BUFS = 10
+RIDERS = 2
 
-F_OFFSET, I_OFFSET, C_OFFSET, SMALL_OFFSET = 0, 4, 8, 12
+ROWS_PER_QUARTER = 4
+SMALL_OFFSET = 12
 
 FLOPS = 2 * B * H * (3 * E + 5 * H)
 
 
-def load_scale_planes(queue, word, planes, offset, scales):
-    rows = scales.bitcast(word).rearrange("g (q r) n -> r q g n", r=4)
-    for r in range(4):
-        queue.dma_start(out=planes[offset + r : P : 32, :, :].bitcast(word), in_=rows[r])
-
-
-def mx_pass(nc, z, act_codes, act_scales, group, words, plane, start, stop):
-    batch_cols = slice(group * B, (group + 1) * B)
-    nc.tensor.matmul_mx(
-        out=z[:],
-        lhsT=act_codes[:, batch_cols].bitcast(FP8X4),
-        lhsT_scale=act_scales[:, batch_cols],
-        rhs=words.bitcast(FP8X4),
-        rhs_scale=plane,
-        start=start,
-        stop=stop,
-    )
-
-
-def stream_x_product(nc, stream, z, words, planes, offset, act_codes, act_scales, chunks, start, stop):
-    by_partition = words.rearrange("g p n t -> p g (n t)").bitcast(I32)
-    for chunk in chunks:
-        first = chunk * CHUNK
-        w_sb = stream.tile([P, CHUNK, H], U32, align_bytes=64)
-        nc.sync.dma_start(out=w_sb[:].bitcast(I32), in_=by_partition[:, first : first + CHUNK, :])
-        for j in range(CHUNK):
-            group = first + j
-            mx_pass(
-                nc, z, act_codes, act_scales, group, w_sb[:, j, :], planes[offset:P, group, :],
-                start=start and group == 0,
-                stop=stop and group == X_GROUPS - 1,
-            )
+def load_scale_rows(queue, word, planes, offset, scales, r):
+    rows = scales.bitcast(word).rearrange("g (q r) n -> r q g n", r=ROWS_PER_QUARTER)
+    queue.dma_start(out=planes[offset + r : P : 32, :, :].bitcast(word), in_=rows[r])
 
 
 def tile_lstm_peephole_build_pa_k_kernel(
@@ -74,6 +48,9 @@ def tile_lstm_peephole_build_pa_k_kernel(
     out,
 ):
     nc = tc.nc
+    F_GATE, I_GATE, C_GATE = range(3)
+    big_words_in = (w_ip_f_words, w_ip_i_words, w_ip_c_dash_words)
+    big_scales_in = (w_ip_f_scales, w_ip_i_scales, w_ip_c_dash_scales)
     FORGET_H, FORGET_C, INPUT_H, INPUT_C, DASH_H = range(5)
     small_words_in = (w_forget_words, w_forget_c_words, w_input_words, w_input_c_words, w_c_dash_words)
     small_scales_in = (w_forget_scales, w_forget_c_scales, w_input_scales, w_input_c_scales, w_c_dash_scales)
@@ -83,6 +60,10 @@ def tile_lstm_peephole_build_pa_k_kernel(
             tc.tile_pool(name="stream", bufs=STREAM_BUFS) as stream, \
             tc.psum_pool(name="sums", bufs=1) as sums, \
             tc.psum_pool(name="turn", bufs=4) as turn:
+
+        warm = keep.tile([P, 1], F32)
+        nc.vector.memset(warm[:], 0.0)
+        nc.scalar.activation(out=warm[:], in_=warm[:], func=ACT.Sigmoid)
 
         acts = keep.tile([P, ACT_GROUPS * K_PASS], BF16, align_bytes=64)
         x_cols = E // X_LOADS
@@ -95,18 +76,22 @@ def tile_lstm_peephole_build_pa_k_kernel(
         nc.sync.dma_start(out=acts[:, c_cols], in_=previous_c_state)
 
         small_planes = keep.tile([P, len(small_scales_in), H], U8, align_bytes=64)
-        f_planes = keep.tile([P, X_GROUPS, H], U8, align_bytes=64)
-        i_planes = keep.tile([P, X_GROUPS, H], U8, align_bytes=64)
-        c_planes = keep.tile([P, X_GROUPS, H], U8, align_bytes=64)
-        for planes in (small_planes, f_planes, i_planes, c_planes):
-            nc.vector.memset(planes[:].bitcast(I32), 0)
-        for slot, scales in enumerate(small_scales_in):
-            load_scale_planes(nc.sync, I32, small_planes[:, slot : slot + 1, :], SMALL_OFFSET, scales)
+        nc.vector.memset(small_planes[:].bitcast(I32), 0)
         ident = keep.tile([P, P], F32)
         make_identity(nc, ident[:])
-        load_scale_planes(nc.gpsimd, F32, f_planes, F_OFFSET, w_ip_f_scales)
-        load_scale_planes(nc.gpsimd, F32, i_planes, I_OFFSET, w_ip_i_scales)
-        load_scale_planes(nc.gpsimd, F32, c_planes, C_OFFSET, w_ip_c_dash_scales)
+        big_planes = []
+        for gate, scales in enumerate(big_scales_in):
+            big_planes.append(keep.tile([P, X_GROUPS, H], U8, name="big_planes%d" % gate, align_bytes=64))
+            nc.vector.memset(big_planes[gate][:].bitcast(I32), 0)
+            for r in range(ROWS_PER_QUARTER):
+                load_scale_rows(nc.gpsimd, F32, big_planes[gate], ROWS_PER_QUARTER * gate, scales, r)
+
+        def small_scale_riders(load):
+            total = ROWS_PER_QUARTER * len(small_scales_in)
+            for n in range(RIDERS * load, min(RIDERS * (load + 1), total)):
+                slot, r = divmod(n, ROWS_PER_QUARTER)
+                load_scale_rows(nc.sync, I32, small_planes[:, slot : slot + 1, :], SMALL_OFFSET,
+                                small_scales_in[slot], r)
 
         act_words = acts[:].bitcast(F32)
         act_codes = keep.tile([P, ACT_GROUPS * B], U32, align_bytes=64)
@@ -134,14 +119,43 @@ def tile_lstm_peephole_build_pa_k_kernel(
                 in_=grouped[:],
             )
 
-        all_chunks = range(X_GROUPS // CHUNK)
+        def mx_pass(z, group, words, plane, start, stop):
+            batch_cols = slice(group * B, (group + 1) * B)
+            nc.tensor.matmul_mx(
+                out=z[:],
+                lhsT=act_codes[:, batch_cols].bitcast(FP8X4),
+                lhsT_scale=act_scales[:, batch_cols],
+                rhs=words.bitcast(FP8X4),
+                rhs_scale=plane,
+                start=start,
+                stop=stop,
+            )
+
+        def x_product(z, gate, first_group, end_group, per_load, start, stop):
+            by_partition = big_words_in[gate].rearrange("g p n t -> p g (n t)").bitcast(I32)
+            for first in range(first_group, end_group, per_load):
+                w_sb = stream.tile([P, CHUNK, H], U32, align_bytes=64)
+                nc.sync.dma_start(
+                    out=w_sb[:, 0:per_load, :].bitcast(I32),
+                    in_=by_partition[:, first : first + per_load, :],
+                )
+                small_scale_riders(gate * LOADS_PER_WEIGHT + first // CHUNK)
+                for j in range(per_load):
+                    group = first + j
+                    mx_pass(
+                        z, group, w_sb[:, j, :], big_planes[gate][ROWS_PER_QUARTER * gate : P, group, :],
+                        start=start and group == 0,
+                        stop=stop and group == X_GROUPS - 1,
+                    )
+
+        def small_pass(z, group, slot, start, stop):
+            mx_pass(z, group, small_words[:, slot, :], small_planes[SMALL_OFFSET:P, slot, :], start, stop)
+
         z_f = sums.tile([B, H], F32)
         z_i = sums.tile([B, H], F32)
         z_c = sums.tile([B, H], F32)
-        stream_x_product(nc, stream, z_f, w_ip_f_words, f_planes, F_OFFSET, act_codes, act_scales,
-                         all_chunks, start=True, stop=False)
-        stream_x_product(nc, stream, z_i, w_ip_i_words, i_planes, I_OFFSET, act_codes, act_scales,
-                         all_chunks, start=True, stop=False)
+        x_product(z_f, F_GATE, 0, X_GROUPS, CHUNK, start=True, stop=False)
+        x_product(z_i, I_GATE, 0, X_GROUPS, CHUNK, start=True, stop=False)
 
         small_words = keep.tile([P, len(small_words_in), H], U32, align_bytes=64)
         for slot, words in enumerate(small_words_in):
@@ -149,16 +163,6 @@ def tile_lstm_peephole_build_pa_k_kernel(
                 out=small_words[:, slot, :].bitcast(I32),
                 in_=words.rearrange("g p n t -> p (g n t)").bitcast(I32),
             )
-
-        def small_pass(z, group, slot, start, stop):
-            mx_pass(
-                nc, z, act_codes, act_scales, group, small_words[:, slot, :],
-                small_planes[SMALL_OFFSET:P, slot, :], start=start, stop=stop,
-            )
-
-        stream_x_product(nc, stream, z_c, w_ip_c_dash_words, c_planes, C_OFFSET, act_codes, act_scales,
-                         all_chunks[:-1], start=True, stop=False)
-
         small_pass(z_f, H_GROUP, FORGET_H, start=False, stop=False)
         small_pass(z_f, C_GROUP, FORGET_C, start=False, stop=True)
         small_pass(z_i, H_GROUP, INPUT_H, start=False, stop=False)
@@ -171,9 +175,9 @@ def tile_lstm_peephole_build_pa_k_kernel(
         admit = keep.tile([B, H], F32)
         nc.scalar.activation(out=admit[:], in_=z_i[:], func=ACT.Sigmoid)
 
-        small_pass(z_c, H_GROUP, DASH_H, start=False, stop=False)
-        stream_x_product(nc, stream, z_c, w_ip_c_dash_words, c_planes, C_OFFSET, act_codes, act_scales,
-                         all_chunks[-1:], start=False, stop=True)
+        small_pass(z_c, H_GROUP, DASH_H, start=True, stop=False)
+        x_product(z_c, C_GATE, 0, X_GROUPS - CHUNK, CHUNK, start=False, stop=False)
+        x_product(z_c, C_GATE, X_GROUPS - CHUNK, X_GROUPS, 1, start=False, stop=True)
 
         fresh = keep.tile([B, H], F32)
         nc.scalar.activation(out=fresh[:], in_=z_c[:], func=ACT.Tanh)

@@ -80,10 +80,11 @@ def tile_lstm_peephole_build_pa_k_kernel(
         ident = keep.tile([P, P], F32)
         make_identity(nc, ident[:])
         big_planes = []
-        for gate, scales in enumerate(big_scales_in):
+        for gate in range(len(big_scales_in)):
             big_planes.append(keep.tile([P, X_GROUPS, H], U8, name="big_planes%d" % gate, align_bytes=64))
             nc.vector.memset(big_planes[gate][:].bitcast(I32), 0)
-            for r in range(ROWS_PER_QUARTER):
+        for r in range(ROWS_PER_QUARTER):
+            for gate, scales in enumerate(big_scales_in):
                 load_scale_rows(nc.gpsimd, F32, big_planes[gate], ROWS_PER_QUARTER * gate, scales, r)
 
         def small_scale_riders(load):

@@ -67,25 +67,30 @@ def tile_lstm_peephole_build_pa_k_kernel(
 
         acts = keep.tile([P, ACT_GROUPS * K_PASS], BF16, align_bytes=64)
         x_cols = E // X_LOADS
-        for i in range(X_LOADS):
+
+        def load_x(i):
             cols = slice(i * x_cols, (i + 1) * x_cols)
             nc.sync.dma_start(out=acts[:, cols], in_=input_data[:, cols])
+
+        load_x(0)
+
+        small_planes = keep.tile([P, len(small_scales_in), H], U8, align_bytes=64)
+        big_planes = keep.tile([P, X_GROUPS, H], U8, align_bytes=64)
+        nc.vector.memset(big_planes[:].bitcast(I32), 0)
+        nc.vector.memset(small_planes[:].bitcast(I32), 0)
+        ident = keep.tile([P, P], F32)
+        make_identity(nc, ident[:])
+        scale_queues = ((nc.sync, I32), (nc.scalar, F32), (nc.gpsimd, F32))
+        for r in range(ROWS_PER_QUARTER):
+            for gate, (queue, word) in enumerate(scale_queues):
+                load_scale_rows(queue, word, big_planes, ROWS_PER_QUARTER * gate, big_scales_in[gate], r)
+
+        for i in range(1, X_LOADS):
+            load_x(i)
         h_cols = slice(H_GROUP * K_PASS, (H_GROUP + 1) * K_PASS)
         c_cols = slice(C_GROUP * K_PASS, (C_GROUP + 1) * K_PASS)
         nc.sync.dma_start(out=acts[:, h_cols], in_=previous_hidden_state)
         nc.sync.dma_start(out=acts[:, c_cols], in_=previous_c_state)
-
-        small_planes = keep.tile([P, len(small_scales_in), H], U8, align_bytes=64)
-        nc.vector.memset(small_planes[:].bitcast(I32), 0)
-        ident = keep.tile([P, P], F32)
-        make_identity(nc, ident[:])
-        big_planes = []
-        for gate in range(len(big_scales_in)):
-            big_planes.append(keep.tile([P, X_GROUPS, H], U8, name="big_planes%d" % gate, align_bytes=64))
-            nc.vector.memset(big_planes[gate][:].bitcast(I32), 0)
-        for r in range(ROWS_PER_QUARTER):
-            for gate, scales in enumerate(big_scales_in):
-                load_scale_rows(nc.gpsimd, F32, big_planes[gate], ROWS_PER_QUARTER * gate, scales, r)
 
         def small_scale_riders(load):
             total = ROWS_PER_QUARTER * len(small_scales_in)
@@ -144,7 +149,7 @@ def tile_lstm_peephole_build_pa_k_kernel(
                 for j in range(per_load):
                     group = first + j
                     mx_pass(
-                        z, group, w_sb[:, j, :], big_planes[gate][ROWS_PER_QUARTER * gate : P, group, :],
+                        z, group, w_sb[:, j, :], big_planes[ROWS_PER_QUARTER * gate : P, group, :],
                         start=start and group == 0,
                         stop=stop and group == X_GROUPS - 1,
                     )

@@ -127,15 +127,18 @@ def tile_lstm_peephole_build_pa_k_kernel(
 
         def mx_pass(z, group, words, plane, start, stop):
             batch_cols = slice(group * B, (group + 1) * B)
-            nc.tensor.matmul_mx(
-                out=z[:],
-                lhsT=act_codes[:, batch_cols].bitcast(FP8X4),
-                lhsT_scale=act_scales[:, batch_cols],
-                rhs=words.bitcast(FP8X4),
-                rhs_scale=plane,
-                start=start,
-                stop=stop,
-            )
+            width = H // len(z)
+            for part, z_part in enumerate(z):
+                cols = slice(part * width, (part + 1) * width)
+                nc.tensor.matmul_mx(
+                    out=z_part[:],
+                    lhsT=act_codes[:, batch_cols].bitcast(FP8X4),
+                    lhsT_scale=act_scales[:, batch_cols],
+                    rhs=words[:, cols].bitcast(FP8X4),
+                    rhs_scale=plane[:, cols],
+                    start=start,
+                    stop=stop,
+                )
 
         def x_product(z, gate, first_group, end_group, per_load, start, stop):
             by_partition = big_words_in[gate].rearrange("g p n t -> p g (n t)").bitcast(I32)
@@ -159,9 +162,11 @@ def tile_lstm_peephole_build_pa_k_kernel(
 
         z_f = sums.tile([B, H], F32)
         z_i = sums.tile([B, H], F32)
-        z_c = sums.tile([B, H], F32)
-        x_product(z_f, F_GATE, 0, X_GROUPS, CHUNK, start=True, stop=False)
-        x_product(z_i, I_GATE, 0, X_GROUPS, CHUNK, start=True, stop=False)
+        z_c0 = sums.tile([B, H // 2], F32)
+        z_c1 = sums.tile([B, H // 2], F32)
+        z_c = (z_c0, z_c1)
+        x_product((z_f,), F_GATE, 0, X_GROUPS, CHUNK, start=True, stop=False)
+        x_product((z_i,), I_GATE, 0, X_GROUPS, CHUNK, start=True, stop=False)
 
         small_words = keep.tile([P, len(small_words_in), H], U32, align_bytes=64)
         for slot, words in enumerate(small_words_in):
@@ -169,10 +174,10 @@ def tile_lstm_peephole_build_pa_k_kernel(
                 out=small_words[:, slot, :].bitcast(I32),
                 in_=words.rearrange("g p n t -> p (g n t)").bitcast(I32),
             )
-        small_pass(z_f, H_GROUP, FORGET_H, start=False, stop=False)
-        small_pass(z_f, C_GROUP, FORGET_C, start=False, stop=True)
-        small_pass(z_i, H_GROUP, INPUT_H, start=False, stop=False)
-        small_pass(z_i, C_GROUP, INPUT_C, start=False, stop=True)
+        small_pass((z_f,), H_GROUP, FORGET_H, start=False, stop=False)
+        small_pass((z_f,), C_GROUP, FORGET_C, start=False, stop=True)
+        small_pass((z_i,), H_GROUP, INPUT_H, start=False, stop=False)
+        small_pass((z_i,), C_GROUP, INPUT_C, start=False, stop=True)
 
         forget = keep.tile([B, H], F32)
         nc.scalar.activation(out=forget[:], in_=z_f[:], func=ACT.Sigmoid)
@@ -186,8 +191,12 @@ def tile_lstm_peephole_build_pa_k_kernel(
         x_product(z_c, C_GATE, X_GROUPS - CHUNK, X_GROUPS, 1, start=False, stop=True)
 
         fresh = keep.tile([B, H], F32)
-        nc.scalar.activation(out=fresh[:], in_=z_c[:], func=ACT.Tanh)
         result = keep.tile([B, H], F32)
-        nc.vector.tensor_mul(out=result[:], in0=admit[:], in1=fresh[:])
-        nc.vector.tensor_add(out=result[:], in0=result[:], in1=kept[:])
-        nc.sync.dma_start(out=out, in_=result[:])
+        halves = [slice(part * H // 2, (part + 1) * H // 2) for part in range(2)]
+        for z_part, cols in zip(z_c, halves):
+            nc.scalar.activation(out=fresh[:, cols], in_=z_part[:], func=ACT.Tanh)
+        for cols in halves:
+            nc.vector.tensor_mul(out=result[:, cols], in0=admit[:, cols], in1=fresh[:, cols])
+        for cols, queue in zip(halves, (nc.sync, nc.scalar)):
+            nc.vector.tensor_add(out=result[:, cols], in0=result[:, cols], in1=kept[:, cols])
+            queue.dma_start(out=out[:, cols], in_=result[:, cols])

@@ -80,10 +80,14 @@ def tile_lstm_peephole_build_pa_k_kernel(
         nc.vector.memset(small_planes[:].bitcast(I32), 0)
         ident = keep.tile([P, P], F32)
         make_identity(nc, ident[:])
-        scale_queues = ((nc.sync, I32), (nc.scalar, F32), (nc.gpsimd, F32))
+        scale_queues = ((nc.sync, I32, 2), (nc.scalar, F32, 2), (nc.gpsimd, F32, 1))
         for r in range(ROWS_PER_QUARTER):
-            for gate, (queue, word) in enumerate(scale_queues):
-                load_scale_rows(queue, word, big_planes, ROWS_PER_QUARTER * gate, big_scales_in[gate], r)
+            for part in range(2):
+                for gate, (queue, word, parts) in enumerate(scale_queues):
+                    if part < parts:
+                        groups = slice(part * X_GROUPS // parts, (part + 1) * X_GROUPS // parts)
+                        load_scale_rows(queue, word, big_planes[:, groups, :], ROWS_PER_QUARTER * gate,
+                                        big_scales_in[gate][groups], r)
 
         for i in range(1, X_LOADS):
             load_x(i)

import concourse.mybir as mybir
from concourse.masks import make_identity

BF16 = mybir.dt.bfloat16
F32 = mybir.dt.float32
I32 = mybir.dt.int32
U32 = mybir.dt.uint32
U8 = mybir.dt.uint8
FP8X4 = mybir.dt.float8_e4m3fn_x4
ACT = mybir.ActivationFunctionType

P = 128
K_PASS = 512
B = 128
H = 512
E = 16384

X_GROUPS = E // K_PASS
H_GROUP = X_GROUPS
C_GROUP = X_GROUPS + 1
ACT_GROUPS = X_GROUPS + 2
X_LOADS = 4

WORDS_PER_GROUP = K_PASS // 2
CHUNK = 4
LOADS_PER_WEIGHT = X_GROUPS // CHUNK
STREAM_BUFS = 10
RIDERS = 2

ROWS_PER_QUARTER = 4
SMALL_OFFSET = 12

FLOPS = 2 * B * H * (3 * E + 5 * H)


def load_scale_rows(queue, word, planes, offset, scales, r):
    rows = scales.bitcast(word).rearrange("g (q r) n -> r q g n", r=ROWS_PER_QUARTER)
    queue.dma_start(out=planes[offset + r : P : 32, :, :].bitcast(word), in_=rows[r])


def tile_lstm_peephole_build_pa_k_kernel(
    tc,
    input_data, previous_hidden_state, previous_c_state,
    w_forget_words, w_forget_scales, w_input_words, w_input_scales,
    w_c_dash_words, w_c_dash_scales, w_forget_c_words, w_forget_c_scales,
    w_input_c_words, w_input_c_scales, w_ip_f_words, w_ip_f_scales,
    w_ip_i_words, w_ip_i_scales, w_ip_c_dash_words, w_ip_c_dash_scales,
    out,
):
    nc = tc.nc
    F_GATE, I_GATE, C_GATE = range(3)
    big_words_in = (w_ip_f_words, w_ip_i_words, w_ip_c_dash_words)
    big_scales_in = (w_ip_f_scales, w_ip_i_scales, w_ip_c_dash_scales)
    FORGET_H, FORGET_C, INPUT_H, INPUT_C, DASH_H = range(5)
    small_words_in = (w_forget_words, w_forget_c_words, w_input_words, w_input_c_words, w_c_dash_words)
    small_scales_in = (w_forget_scales, w_forget_c_scales, w_input_scales, w_input_c_scales, w_c_dash_scales)

    with tc.tile_pool(name="keep", bufs=1) as keep, \
            tc.tile_pool(name="stage", bufs=4) as stage, \
            tc.tile_pool(name="stream", bufs=STREAM_BUFS) as stream, \
            tc.psum_pool(name="sums", bufs=1) as sums, \
            tc.psum_pool(name="turn", bufs=4) as turn:

        warm = keep.tile([P, 1], F32)
        nc.vector.memset(warm[:], 0.0)
        nc.scalar.activation(out=warm[:], in_=warm[:], func=ACT.Sigmoid)

        acts = keep.tile([P, ACT_GROUPS * K_PASS], BF16, align_bytes=64)
        x_cols = E // X_LOADS

        def load_x(i):
            cols = slice(i * x_cols, (i + 1) * x_cols)
            nc.sync.dma_start(out=acts[:, cols], in_=input_data[:, cols])

        load_x(0)

        small_planes = keep.tile([P, len(small_scales_in), H], U8, align_bytes=64)
        big_planes = keep.tile([P, X_GROUPS, H], U8, align_bytes=64)
        nc.vector.memset(big_planes[:].bitcast(I32), 0)
        nc.vector.memset(small_planes[:].bitcast(I32), 0)
        ident = keep.tile([P, P], F32)
        make_identity(nc, ident[:])
        scale_queues = ((nc.sync, I32, 2), (nc.scalar, F32, 2), (nc.gpsimd, F32, 1))
        for r in range(ROWS_PER_QUARTER):
            for part in range(2):
                for gate, (queue, word, parts) in enumerate(scale_queues):
                    if part < parts:
                        groups = slice(part * X_GROUPS // parts, (part + 1) * X_GROUPS // parts)
                        load_scale_rows(queue, word, big_planes[:, groups, :], ROWS_PER_QUARTER * gate,
                                        big_scales_in[gate][groups], r)

        for i in range(1, X_LOADS):
            load_x(i)
        h_cols = slice(H_GROUP * K_PASS, (H_GROUP + 1) * K_PASS)
        c_cols = slice(C_GROUP * K_PASS, (C_GROUP + 1) * K_PASS)
        nc.sync.dma_start(out=acts[:, h_cols], in_=previous_hidden_state)
        nc.sync.dma_start(out=acts[:, c_cols], in_=previous_c_state)

        def small_scale_riders(load):
            total = ROWS_PER_QUARTER * len(small_scales_in)
            for n in range(RIDERS * load, min(RIDERS * (load + 1), total)):
                slot, r = divmod(n, ROWS_PER_QUARTER)
                load_scale_rows(nc.sync, I32, small_planes[:, slot : slot + 1, :], SMALL_OFFSET,
                                small_scales_in[slot], r)

        act_words = acts[:].bitcast(F32)
        act_codes = keep.tile([P, ACT_GROUPS * B], U32, align_bytes=64)
        act_scales = keep.tile([P, ACT_GROUPS * B], U8, align_bytes=64)
        for pair in range(ACT_GROUPS // 2):
            turned = turn.tile([P, 2, 2, B], F32)
            for gg in range(2):
                first_word = (2 * pair + gg) * WORDS_PER_GROUP
                for u in range(2):
                    nc.tensor.transpose(
                        turned[:, gg, u, :],
                        act_words[:, first_word + u : first_word + WORDS_PER_GROUP : 2],
                        ident[:],
                    )
            grouped = stage.tile([P, 2 * K_PASS], BF16, align_bytes=64)
            copy_out = nc.vector.tensor_copy if pair % 2 == 0 else nc.scalar.copy
            copy_out(
                out=grouped[:].bitcast(F32).rearrange("p (gg b u) -> p gg b u", gg=2, u=2),
                in_=turned[:].rearrange("p gg u b -> p gg b u"),
            )
            pair_cols = slice(2 * pair * B, (2 * pair + 2) * B)
            nc.vector.quantize_mx(
                out=act_codes[:, pair_cols].bitcast(FP8X4),
                scales=act_scales[:, pair_cols],
                in_=grouped[:],
            )

        def mx_pass(z, group, words, plane, start, stop):
            batch_cols = slice(group * B, (group + 1) * B)
            width = H // len(z)
            for part, z_part in enumerate(z):
                cols = slice(part * width, (part + 1) * width)
                nc.tensor.matmul_mx(
                    out=z_part[:],
                    lhsT=act_codes[:, batch_cols].bitcast(FP8X4),
                    lhsT_scale=act_scales[:, batch_cols],
                    rhs=words[:, cols].bitcast(FP8X4),
                    rhs_scale=plane[:, cols],
                    start=start,
                    stop=stop,
                )

        def x_product(z, gate, first_group, end_group, per_load, start, stop):
            by_partition = big_words_in[gate].rearrange("g p n t -> p g (n t)").bitcast(I32)
            for first in range(first_group, end_group, per_load):
                w_sb = stream.tile([P, CHUNK, H], U32, align_bytes=64)
                nc.sync.dma_start(
                    out=w_sb[:, 0:per_load, :].bitcast(I32),
                    in_=by_partition[:, first : first + per_load, :],
                )
                small_scale_riders(gate * LOADS_PER_WEIGHT + first // CHUNK)
                for j in range(per_load):
                    group = first + j
                    mx_pass(
                        z, group, w_sb[:, j, :], big_planes[ROWS_PER_QUARTER * gate : P, group, :],
                        start=start and group == 0,
                        stop=stop and group == X_GROUPS - 1,
                    )

        def small_pass(z, group, slot, start, stop):
            mx_pass(z, group, small_words[:, slot, :], small_planes[SMALL_OFFSET:P, slot, :], start, stop)

        z_f = sums.tile([B, H], F32)
        z_i = sums.tile([B, H], F32)
        z_c0 = sums.tile([B, H // 2], F32)
        z_c1 = sums.tile([B, H // 2], F32)
        z_c = (z_c0, z_c1)
        x_product((z_f,), F_GATE, 0, X_GROUPS, CHUNK, start=True, stop=False)
        x_product((z_i,), I_GATE, 0, X_GROUPS, CHUNK, start=True, stop=False)

        small_words = keep.tile([P, len(small_words_in), H], U32, align_bytes=64)
        for slot, words in enumerate(small_words_in):
            nc.sync.dma_start(
                out=small_words[:, slot, :].bitcast(I32),
                in_=words.rearrange("g p n t -> p (g n t)").bitcast(I32),
            )
        small_pass((z_f,), H_GROUP, FORGET_H, start=False, stop=False)
        small_pass((z_f,), C_GROUP, FORGET_C, start=False, stop=True)
        small_pass((z_i,), H_GROUP, INPUT_H, start=False, stop=False)
        small_pass((z_i,), C_GROUP, INPUT_C, start=False, stop=True)

        forget = keep.tile([B, H], F32)
        nc.scalar.activation(out=forget[:], in_=z_f[:], func=ACT.Sigmoid)
        kept = keep.tile([B, H], F32)
        nc.vector.tensor_mul(out=kept[:], in0=forget[:], in1=acts[:, c_cols])
        admit = keep.tile([B, H], F32)
        nc.scalar.activation(out=admit[:], in_=z_i[:], func=ACT.Sigmoid)

        small_pass(z_c, H_GROUP, DASH_H, start=True, stop=False)
        x_product(z_c, C_GATE, 0, X_GROUPS - CHUNK, CHUNK, start=False, stop=False)
        x_product(z_c, C_GATE, X_GROUPS - CHUNK, X_GROUPS, 1, start=False, stop=True)

        fresh = keep.tile([B, H], F32)
        result = keep.tile([B, H], F32)
        halves = [slice(part * H // 2, (part + 1) * H // 2) for part in range(2)]
        for z_part, cols in zip(z_c, halves):
            nc.scalar.activation(out=fresh[:, cols], in_=z_part[:], func=ACT.Tanh)
        for cols in halves:
            nc.vector.tensor_mul(out=result[:, cols], in0=admit[:, cols], in1=fresh[:, cols])
        for cols, queue in zip(halves, (nc.sync, nc.scalar)):
            nc.vector.tensor_add(out=result[:, cols], in0=result[:, cols], in1=kept[:, cols])
            queue.dma_start(out=out[:, cols], in_=result[:, cols])
